import numpy as np
import ml_dtypes


def mxq(x, axis, fmt="e4m3"):
    dtype, down = {"e4m3": (ml_dtypes.float8_e4m3fn, 7), "e5m2": (ml_dtypes.float8_e5m2, 14)}[fmt]
    v = np.moveaxis(np.asarray(x, np.float32).astype(ml_dtypes.bfloat16).astype(np.float64), axis, -1)
    blocks = v.reshape(v.shape[:-1] + (-1, 32))
    amax = np.abs(blocks).max(-1, keepdims=True)
    byte = np.maximum(np.where(amax > 0, np.frexp(amax)[1] - 1 + 127, 0) - down, 1)
    scale = np.exp2(byte - 127.0)
    codes = (blocks / scale).astype(np.float32).astype(dtype).astype(np.float64)
    return np.moveaxis((codes * scale).reshape(v.shape), -1, axis)


WIDE = False


def mx_kscale(k):
    if not WIDE:
        return np.ones(k)
    levels = np.array([10, -10, 5, -5, 0])
    if k % 512:
        return np.exp2(np.random.permutation(np.resize(levels, k // 32))).repeat(32)
    a = np.empty((k // 512, 16))
    for p in range(k // 512):
        a[p, :8] = np.random.permutation(np.resize(levels, 8))
        for g in range(8):
            far = levels[np.abs(levels - a[p, g]) >= 10]
            a[p, g + 8] = far[np.random.randint(len(far))]
    return np.exp2(a.ravel()).repeat(32)


BF16 = ml_dtypes.bfloat16


def bf(x):
    return np.asarray(x, np.float32).astype(BF16)


def f64(x):
    return np.asarray(x).astype(np.float64)


B, S, HID, H, HK, D = 2, 256, 2048, 16, 4, 128
EPS = 1e-6
PRE = 0.004


def rmsnorm(v, w):
    var = np.mean(v * v, axis=-1, keepdims=True)
    return w * (v * (1.0 / np.sqrt(var + EPS)))


def rope(v, cos, sin):
    c = cos[:, :, None, :]
    sn = sin[:, :, None, :]
    v1, v2 = np.split(v, 2, axis=-1)
    rot = np.concatenate([-v2, v1], axis=-1)
    return v * c + rot * sn


def setup_inputs():
    s = mx_kscale(HID)
    return {
        "hidden_states": bf(np.random.standard_normal((B, S, HID)) * s),
        "cos": bf(np.cos(np.random.standard_normal((B, S, D)))),
        "sin": bf(np.sin(np.random.standard_normal((B, S, D)))),
        "Wq_query": bf(np.random.standard_normal((H * D, HID)) * PRE / np.sqrt(HID) / s),
        "Wk": bf(np.random.standard_normal((HK * D, HID)) * PRE / np.sqrt(HID) / s),
        "q_norm_w": bf(1.0 + 0.1 * np.random.standard_normal(D)),
        "k_norm_w": bf(1.0 + 0.1 * np.random.standard_normal(D)),
    }


def reference(hidden_states, cos, sin, Wq_query, Wk, q_norm_w, k_norm_w):
    xq = mxq(f64(hidden_states), 2, "e4m3")
    q = (xq @ mxq(f64(Wq_query), 1, "e4m3").T).reshape(B, S, H, D)
    k = (xq @ mxq(f64(Wk), 1, "e4m3").T).reshape(B, S, HK, D)
    q = rmsnorm(q, f64(q_norm_w))
    k = rmsnorm(k, f64(k_norm_w))
    q = rope(q, f64(cos), f64(sin))
    k = rope(k, f64(cos), f64(sin))
    return q, k

@@ -1,0 +1,222 @@
+from contextlib import ExitStack
+
+import concourse.mybir as mybir
+from concourse.masks import make_identity
+
+F32 = mybir.dt.float32
+BF16 = mybir.dt.bfloat16
+U32 = mybir.dt.uint32
+U8 = mybir.dt.uint8
+FP8X4 = mybir.dt.float8_e4m3fn_x4
+ACT = mybir.ActivationFunctionType
+ALU = mybir.AluOpType
+
+P = 128
+PACK = 4
+HIDDEN = 2048
+PASSES = HIDDEN // (P * PACK)
+WORDS = HIDDEN // 2
+BLOCK = 512
+HALF = BLOCK // 2
+HEAD = 128
+TOKEN_TILES = 4
+EPS = 1e-6
+STEPS_PER_TURN = 2
+
+FLOPS = 2 * 512 * (2048 + 512) * HIDDEN
+
+
+def tile_qwen3nextattentionforengine_pa_kernel(
+    tc, hidden_states, cos, sin, Wq_query, Wk, q_norm_w, k_norm_w, out_0, out_1
+):
+    nc = tc.nc
+    tokens = hidden_states.rearrange("b s k -> (b s) k")
+    q_flat = out_0.rearrange("b s h d -> (b s) (h d)")
+    k_flat = out_1.rearrange("b s h d -> (b s) (h d)")
+
+    blocks = []
+    for first, width in ((0, HALF), (HALF, HALF), (512, BLOCK), (1024, BLOCK), (1536, BLOCK)):
+        blocks.append((Wq_query[first : first + width, :], q_flat[:, first : first + width], 0))
+    blocks.append((Wk, k_flat, 1))
+
+    halves = [("x", 0), (0, 0), ("x", 1), (1, 0)]
+    halves += [(b, h) for b in range(2, len(blocks)) for h in range(2)]
+    jobs = [(owner, h, g) for owner, h in halves for g in (0, 2)]
+    HEAD_JOBS = 4
+
+    with ExitStack() as ctx:
+        consts = ctx.enter_context(tc.tile_pool(name="consts", bufs=1))
+        raw_pool = ctx.enter_context(tc.tile_pool(name="raw", bufs=len(halves)))
+        group_pool = ctx.enter_context(tc.tile_pool(name="grouped", bufs=6))
+        weight_pool = ctx.enter_context(tc.tile_pool(name="weights", bufs=2))
+        small_pool = ctx.enter_context(tc.tile_pool(name="small", bufs=4))
+        prod_pool = ctx.enter_context(tc.tile_pool(name="prod", bufs=4))
+        result_pool = ctx.enter_context(tc.tile_pool(name="result", bufs=len(blocks) * TOKEN_TILES))
+        turn_psum = ctx.enter_context(tc.psum_pool(name="turn", bufs=4))
+        acc_psum = ctx.enter_context(tc.psum_pool(name="acc", bufs=4))
+        ctx.enter_context(tc.manual_schedule())
+
+        eps_col = consts.tile([P, 1], F32, name="eps_col")
+        nc.vector.memset(eps_col[:], EPS)
+        gain_rows = consts.tile([P, 2 * HEAD], BF16, name="gain_rows")
+        nc.vector.memset(gain_rows[:], 0.0)
+        ones = consts.tile([P, P], BF16, name="ones")
+        nc.vector.memset(ones[:], 1.0)
+        ident = consts.tile([P, P], F32, name="ident")
+        make_identity(nc, ident[:])
+        warm = consts.tile([P, 1], F32, name="warm")
+        nc.scalar.activation(out=warm[:], in_=eps_col[:], func=ACT.Abs_reciprocal_sqrt)
+
+        raws = {}
+
+        def load_half(owner, h):
+            rows = tokens if owner == "x" else blocks[owner][0]
+            raw = raw_pool.tile([P, 2 * HIDDEN], BF16, name="raw")
+            nc.sync.dma_start(
+                out=raw[:], in_=rows[HALF * h : HALF * (h + 1), :].rearrange("(p r) k -> p (r k)", r=2)
+            )
+            raws[(owner, h)] = raw
+
+        cos_sb = consts.tile([P, TOKEN_TILES, HEAD], BF16, name="cos_sb")
+        sin_sb = consts.tile([P, TOKEN_TILES, HEAD], BF16, name="sin_sb")
+        for owner, h in halves[:3]:
+            load_half(owner, h)
+        nc.sync.dma_start(out=gain_rows[0:1, 0:HEAD], in_=q_norm_w.unsqueeze(0))
+        nc.sync.dma_start(out=gain_rows[0:1, HEAD : 2 * HEAD], in_=k_norm_w.unsqueeze(0))
+        nc.sync.dma_start(out=cos_sb[:], in_=cos.rearrange("b (t p) d -> p (b t) d", p=P))
+        nc.sync.dma_start(out=sin_sb[:], in_=sin.rearrange("b (t p) d -> p (b t) d", p=P))
+        for owner, h in halves[3:]:
+            load_half(owner, h)
+
+        tables = consts.tile([P, 2, TOKEN_TILES, 2, HEAD], F32, name="tables")
+        LOW = slice(0, HEAD // 2)
+        HIGH = slice(HEAD // 2, HEAD)
+
+        def build_tables():
+            gains = acc_psum.tile([P, 2 * HEAD], F32, name="acc")
+            nc.tensor.matmul(out=gains[:], lhsT=ones[:], rhs=gain_rows[:], start=True, stop=True)
+            for n in range(2):
+                gain = gains[:, HEAD * n : HEAD * (n + 1)].unsqueeze(1)
+                nc.vector.tensor_tensor(
+                    out=tables[:, n, :, 0, :],
+                    in0=cos_sb[:],
+                    in1=gain.to_broadcast([P, TOKEN_TILES, HEAD]),
+                    op=ALU.mult,
+                )
+                for here, there, sign in ((LOW, HIGH, 1.0), (HIGH, LOW, -1.0)):
+                    nc.vector.scalar_tensor_tensor(
+                        out=tables[:, n, :, 1, here],
+                        in0=sin_sb[:, :, there],
+                        scalar=sign,
+                        in1=gain[:, :, here].to_broadcast([P, TOKEN_TILES, HEAD // 2]),
+                        op0=ALU.mult,
+                        op1=ALU.mult,
+                    )
+
+        operands = {}
+        packed = set()
+
+        def turn(job):
+            owner, h, first_pass = job
+            if owner not in operands:
+                pool = consts if owner == "x" else weight_pool
+                codes = pool.tile([P, PASSES, BLOCK], U32, align_bytes=64, name="codes")
+                scales = pool.tile([P, PASSES, BLOCK], U8, align_bytes=64, name="scales")
+                operands[owner] = (codes, scales)
+            words = raws[(owner, h)][:].bitcast(F32)
+            banks = []
+            for g in (first_pass, first_pass + 1):
+                bank = turn_psum.tile([P, 2, 2, P], F32, name="bank")
+                for u in range(2):
+                    for r in range(2):
+                        first = WORDS * r + 2 * P * g
+                        picked = words[:, first + u : first + 2 * P : 2]
+                        nc.tensor.transpose(bank[:, u, r, :], picked, ident[:])
+                banks.append(bank)
+            return banks
+
+        def pack(job, banks):
+            owner, h, first_pass = job
+            codes, scales = operands[owner]
+            rows = slice(HALF * h, HALF * (h + 1))
+            grouped_pair = []
+            for bank in banks:
+                grouped = group_pool.tile([P, PACK * HALF], BF16, align_bytes=64, name="grouped")
+                nc.scalar.copy(
+                    out=grouped[:].bitcast(F32).rearrange("p (c r u) -> p c r u", r=2, u=2),
+                    in_=bank[:].rearrange("p u r c -> p c r u"),
+                )
+                grouped_pair.append(grouped)
+            for g, grouped in zip((first_pass, first_pass + 1), grouped_pair):
+                nc.vector.quantize_mx(
+                    out=codes[:, g, rows].bitcast(FP8X4), scales=scales[:, g, rows], in_=grouped[:]
+                )
+            packed.add(job)
+
+        def project(b, t):
+            width = blocks[b][0].shape[0]
+            needed = [("x", t // 2, g) for g in (0, 2)]
+            needed += [(b, h, g) for h in range(width // HALF) for g in (0, 2)]
+            assert all(job in packed for job in needed)
+            x_codes, x_scales = operands["x"]
+            w_codes, w_scales = operands[b]
+            toks = slice(P * t, P * (t + 1))
+            acc = acc_psum.tile([P, width], F32, name="acc")
+            for g in range(PASSES):
+                nc.tensor.matmul_mx(
+                    out=acc[:],
+                    lhsT=x_codes[:, g, toks].bitcast(FP8X4),
+                    lhsT_scale=x_scales[:, g, toks],
+                    rhs=w_codes[:, g, 0:width].bitcast(FP8X4),
+                    rhs_scale=w_scales[:, g, 0:width],
+                    start=(g == 0),
+                    stop=(g == PASSES - 1),
+                )
+            return acc
+
+        def finish(b, t, acc):
+            rows, target, n = blocks[b]
+            width = rows.shape[0]
+            heads = width // HEAD
+            squares = small_pool.tile([P, width], BF16, name="squares")
+            sums = small_pool.tile([P, heads], F32, name="sums")
+            for hd in range(heads):
+                cols = slice(HEAD * hd, HEAD * (hd + 1))
+                nc.scalar.activation(
+                    out=squares[:, cols], in_=acc[:, cols], func=ACT.Square, accum_out=sums[:, hd : hd + 1]
+                )
+            inv_rms = small_pool.tile([P, heads], F32, name="inv_rms")
+            nc.scalar.activation(
+                out=inv_rms[:], in_=sums[:], func=ACT.Abs_reciprocal_sqrt, bias=eps_col[:], scale=1.0 / HEAD
+            )
+            prod = prod_pool.tile([P, heads, 2, HEAD], F32, name="prod")
+            for hd in range(heads):
+                nc.vector.scalar_tensor_tensor(
+                    out=prod[:, hd, :, :],
+                    in0=acc[:, HEAD * hd : HEAD * (hd + 1)].unsqueeze(1).to_broadcast([P, 2, HEAD]),
+                    scalar=inv_rms[:, hd : hd + 1],
+                    in1=tables[:, n, t, :, :],
+                    op0=ALU.mult,
+                    op1=ALU.mult,
+                )
+            result = result_pool.tile([P, heads, 2, HEAD // 2], F32, name="result")
+            stay = prod[:, :, 0, :].rearrange("p h (s d) -> p h s d", s=2)
+            cross = prod[:, :, 1, :].rearrange("p h (s d) -> p h s d", s=2)
+            nc.gpsimd.tensor_tensor(out=result[:], in0=stay, in1=cross[:, :, ::-1, :], op=ALU.add)
+            nc.sync.dma_start(out=target[P * t : P * (t + 1), :], in_=result[:].rearrange("p h s d -> p (h s d)"))
+
+        for job in jobs[:HEAD_JOBS]:
+            pack(job, turn(job))
+        build_tables()
+
+        later_jobs = jobs[HEAD_JOBS:]
+        steps = [(b, t) for b in range(len(blocks)) for t in range(TOKEN_TILES)]
+        for first in range(0, len(steps), STEPS_PER_TURN):
+            turn_steps = steps[first : first + STEPS_PER_TURN]
+            turn_jobs = later_jobs[first : first + STEPS_PER_TURN]
+            turned = [turn(job) for job in turn_jobs]
+            accs = [project(b, t) for b, t in turn_steps]
+            for job, banks in zip(turn_jobs, turned):
+                pack(job, banks)
+            for (b, t), acc in zip(turn_steps, accs):
+                finish(b, t, acc)

@@ -69,18 +69,21 @@ def tile_qwen3nextattentionforengine_pa_kernel(
 
         raws = {}
 
-        def load_half(owner, h):
+        def load_half(owner, h, pieces=1):
             rows = tokens if owner == "x" else blocks[owner][0]
-            raw = raw_pool.tile([P, 2 * HIDDEN], BF16, name="raw")
-            nc.sync.dma_start(
-                out=raw[:], in_=rows[HALF * h : HALF * (h + 1), :].rearrange("(p r) k -> p (r k)", r=2)
-            )
+            source = rows[HALF * h : HALF * (h + 1), :].rearrange("(p r) k -> p r k", r=2)
+            raw = raw_pool.tile([P, 2, HIDDEN], BF16, name="raw")
+            width = HIDDEN // pieces
+            for first in range(0, HIDDEN, width):
+                cols = slice(first, first + width)
+                nc.sync.dma_start(out=raw[:, :, cols], in_=source[:, :, cols])
             raws[(owner, h)] = raw
 
         cos_sb = consts.tile([P, TOKEN_TILES, HEAD], BF16, name="cos_sb")
         sin_sb = consts.tile([P, TOKEN_TILES, HEAD], BF16, name="sin_sb")
-        for owner, h in halves[:3]:
-            load_half(owner, h)
+        load_half(*halves[0], pieces=PASSES)
+        load_half(*halves[1], pieces=2)
+        load_half(*halves[2])
         nc.sync.dma_start(out=gain_rows[0:1, 0:HEAD], in_=q_norm_w.unsqueeze(0))
         nc.sync.dma_start(out=gain_rows[0:1, HEAD : 2 * HEAD], in_=k_norm_w.unsqueeze(0))
         nc.sync.dma_start(out=cos_sb[:], in_=cos.rearrange("b (t p) d -> p (b t) d", p=P))
@@ -123,7 +126,7 @@ def tile_qwen3nextattentionforengine_pa_kernel(
                 codes = pool.tile([P, PASSES, BLOCK], U32, align_bytes=64, name="codes")
                 scales = pool.tile([P, PASSES, BLOCK], U8, align_bytes=64, name="scales")
                 operands[owner] = (codes, scales)
-            words = raws[(owner, h)][:].bitcast(F32)
+            words = raws[(owner, h)][:].rearrange("p r k -> p (r k)").bitcast(F32)
             banks = []
             for g in (first_pass, first_pass + 1):
                 bank = turn_psum.tile([P, 2, 2, P], F32, name="bank")

@@ -71,7 +71,7 @@ def tile_qwen3nextattentionforengine_pa_kernel(
 
         def load_half(owner, h, pieces=1):
             rows = tokens if owner == "x" else blocks[owner][0]
-            source = rows[HALF * h : HALF * (h + 1), :].rearrange("(p r) k -> p r k", r=2)
+            source = rows[HALF * h : HALF * (h + 1), :].rearrange("(r p) k -> p r k", r=2)
             raw = raw_pool.tile([P, 2, HIDDEN], BF16, name="raw")
             width = HIDDEN // pieces
             for first in range(0, HIDDEN, width):
@@ -146,8 +146,8 @@ def tile_qwen3nextattentionforengine_pa_kernel(
             for bank in banks:
                 grouped = group_pool.tile([P, PACK * HALF], BF16, align_bytes=64, name="grouped")
                 nc.scalar.copy(
-                    out=grouped[:].bitcast(F32).rearrange("p (c r u) -> p c r u", r=2, u=2),
-                    in_=bank[:].rearrange("p u r c -> p c r u"),
+                    out=grouped[:].bitcast(F32).rearrange("p (r c u) -> p r c u", r=2, u=2),
+                    in_=bank[:].rearrange("p u r c -> p r c u"),
                 )
                 grouped_pair.append(grouped)
             for g, grouped in zip((first_pass, first_pass + 1), grouped_pair):

@@ -15,13 +15,14 @@ P = 128
 PACK = 4
 HIDDEN = 2048
 PASSES = HIDDEN // (P * PACK)
-WORDS = HIDDEN // 2
 BLOCK = 512
 HALF = BLOCK // 2
 HEAD = 128
 TOKEN_TILES = 4
 EPS = 1e-6
 STEPS_PER_TURN = 2
+AHEAD = 2
+ORDERED_JOBS = 1
 
 FLOPS = 2 * 512 * (2048 + 512) * HIDDEN
 
@@ -46,7 +47,8 @@ def tile_qwen3nextattentionforengine_pa_kernel(
 
     with ExitStack() as ctx:
         consts = ctx.enter_context(tc.tile_pool(name="consts", bufs=1))
-        raw_pool = ctx.enter_context(tc.tile_pool(name="raw", bufs=len(halves)))
+        raw_pool = ctx.enter_context(tc.tile_pool(name="raw", bufs=len(halves) - 2))
+        order_pool = ctx.enter_context(tc.tile_pool(name="ordered", bufs=8))
         group_pool = ctx.enter_context(tc.tile_pool(name="grouped", bufs=6))
         weight_pool = ctx.enter_context(tc.tile_pool(name="weights", bufs=2))
         small_pool = ctx.enter_context(tc.tile_pool(name="small", bufs=4))
@@ -72,12 +74,16 @@ def tile_qwen3nextattentionforengine_pa_kernel(
         def load_half(owner, h, pieces=1):
             rows = tokens if owner == "x" else blocks[owner][0]
             source = rows[HALF * h : HALF * (h + 1), :].rearrange("(r p) k -> p r k", r=2)
-            raw = raw_pool.tile([P, 2, HIDDEN], BF16, name="raw")
             width = HIDDEN // pieces
             for first in range(0, HIDDEN, width):
-                cols = slice(first, first + width)
-                nc.sync.dma_start(out=raw[:, :, cols], in_=source[:, :, cols])
-            raws[(owner, h)] = raw
+                if pieces == 1:
+                    raw = raw_pool.tile([P, 2, HIDDEN], BF16, name="raw")
+                else:
+                    raw = consts.tile([P, 2, width], BF16, name=f"raw_{owner}_{first}")
+                nc.sync.dma_start(out=raw[:], in_=source[:, :, first : first + width])
+                words = raw[:].bitcast(F32)
+                for i in range(PASSES // pieces):
+                    raws[(owner, h, first // (P * PACK) + i)] = words[:, :, 2 * P * i : 2 * P * (i + 1)]
 
         cos_sb = consts.tile([P, TOKEN_TILES, HEAD], BF16, name="cos_sb")
         sin_sb = consts.tile([P, TOKEN_TILES, HEAD], BF16, name="sin_sb")
@@ -119,6 +125,18 @@ def tile_qwen3nextattentionforengine_pa_kernel(
         operands = {}
         packed = set()
 
+        ordered = {}
+
+        def put_in_order(job):
+            owner, h, first_pass = job
+            for g in (first_pass, first_pass + 1):
+                unit = order_pool.tile([P, 2, 2, P], F32, name="unit")
+                nc.vector.tensor_copy(
+                    out=unit[:],
+                    in_=raws[(owner, h, g)].rearrange("c r (p u) -> c r u p", u=2),
+                )
+                ordered[(job, g)] = unit
+
         def turn(job):
             owner, h, first_pass = job
             if owner not in operands:
@@ -126,14 +144,15 @@ def tile_qwen3nextattentionforengine_pa_kernel(
                 codes = pool.tile([P, PASSES, BLOCK], U32, align_bytes=64, name="codes")
                 scales = pool.tile([P, PASSES, BLOCK], U8, align_bytes=64, name="scales")
                 operands[owner] = (codes, scales)
-            words = raws[(owner, h)][:].rearrange("p r k -> p (r k)").bitcast(F32)
             banks = []
             for g in (first_pass, first_pass + 1):
                 bank = turn_psum.tile([P, 2, 2, P], F32, name="bank")
                 for u in range(2):
                     for r in range(2):
-                        first = WORDS * r + 2 * P * g
-                        picked = words[:, first + u : first + 2 * P : 2]
+                        if (job, g) in ordered:
+                            picked = ordered[(job, g)][:, r, u, :]
+                        else:
+                            picked = raws[(owner, h, g)][:, r, u : 2 * P : 2]
                         nc.tensor.transpose(bank[:, u, r, :], picked, ident[:])
                 banks.append(bank)
             return banks
@@ -217,9 +236,13 @@ def tile_qwen3nextattentionforengine_pa_kernel(
         for first in range(0, len(steps), STEPS_PER_TURN):
             turn_steps = steps[first : first + STEPS_PER_TURN]
             turn_jobs = later_jobs[first : first + STEPS_PER_TURN]
+            coming = first + AHEAD * STEPS_PER_TURN
+            coming_jobs = later_jobs[coming : coming + ORDERED_JOBS] if first >= STEPS_PER_TURN else []
             turned = [turn(job) for job in turn_jobs]
             accs = [project(b, t) for b, t in turn_steps]
             for job, banks in zip(turn_jobs, turned):
                 pack(job, banks)
+            for job in coming_jobs:
+                put_in_order(job)
             for (b, t), acc in zip(turn_steps, accs):
                 finish(b, t, acc)

@@ -21,8 +21,6 @@ HEAD = 128
 TOKEN_TILES = 4
 EPS = 1e-6
 STEPS_PER_TURN = 2
-AHEAD = 2
-ORDERED_JOBS = 1
 
 FLOPS = 2 * 512 * (2048 + 512) * HIDDEN
 
@@ -48,7 +46,6 @@ def tile_qwen3nextattentionforengine_pa_kernel(
     with ExitStack() as ctx:
         consts = ctx.enter_context(tc.tile_pool(name="consts", bufs=1))
         raw_pool = ctx.enter_context(tc.tile_pool(name="raw", bufs=len(halves) - 2))
-        order_pool = ctx.enter_context(tc.tile_pool(name="ordered", bufs=8))
         group_pool = ctx.enter_context(tc.tile_pool(name="grouped", bufs=6))
         weight_pool = ctx.enter_context(tc.tile_pool(name="weights", bufs=2))
         small_pool = ctx.enter_context(tc.tile_pool(name="small", bufs=4))
@@ -125,18 +122,6 @@ def tile_qwen3nextattentionforengine_pa_kernel(
         operands = {}
         packed = set()
 
-        ordered = {}
-
-        def put_in_order(job):
-            owner, h, first_pass = job
-            for g in (first_pass, first_pass + 1):
-                unit = order_pool.tile([P, 2, 2, P], F32, name="unit")
-                nc.vector.tensor_copy(
-                    out=unit[:],
-                    in_=raws[(owner, h, g)].rearrange("c r (p u) -> c r u p", u=2),
-                )
-                ordered[(job, g)] = unit
-
         def turn(job):
             owner, h, first_pass = job
             if owner not in operands:
@@ -149,10 +134,7 @@ def tile_qwen3nextattentionforengine_pa_kernel(
                 bank = turn_psum.tile([P, 2, 2, P], F32, name="bank")
                 for u in range(2):
                     for r in range(2):
-                        if (job, g) in ordered:
-                            picked = ordered[(job, g)][:, r, u, :]
-                        else:
-                            picked = raws[(owner, h, g)][:, r, u : 2 * P : 2]
+                        picked = raws[(owner, h, g)][:, r, u : 2 * P : 2]
                         nc.tensor.transpose(bank[:, u, r, :], picked, ident[:])
                 banks.append(bank)
             return banks
@@ -221,28 +203,36 @@ def tile_qwen3nextattentionforengine_pa_kernel(
                     op0=ALU.mult,
                     op1=ALU.mult,
                 )
+            return prod
+
+        def add_and_store(b, t, prod, engine):
+            rows, target, n = blocks[b]
+            heads = rows.shape[0] // HEAD
             result = result_pool.tile([P, heads, 2, HEAD // 2], F32, name="result")
             stay = prod[:, :, 0, :].rearrange("p h (s d) -> p h s d", s=2)
             cross = prod[:, :, 1, :].rearrange("p h (s d) -> p h s d", s=2)
-            nc.gpsimd.tensor_tensor(out=result[:], in0=stay, in1=cross[:, :, ::-1, :], op=ALU.add)
+            engine.tensor_tensor(out=result[:], in0=stay, in1=cross[:, :, ::-1, :], op=ALU.add)
             nc.sync.dma_start(out=target[P * t : P * (t + 1), :], in_=result[:].rearrange("p h s d -> p (h s d)"))
 
         for job in jobs[:HEAD_JOBS]:
             pack(job, turn(job))
-        build_tables()
 
         later_jobs = jobs[HEAD_JOBS:]
         steps = [(b, t) for b in range(len(blocks)) for t in range(TOKEN_TILES)]
+        unadded = []
         for first in range(0, len(steps), STEPS_PER_TURN):
             turn_steps = steps[first : first + STEPS_PER_TURN]
             turn_jobs = later_jobs[first : first + STEPS_PER_TURN]
-            coming = first + AHEAD * STEPS_PER_TURN
-            coming_jobs = later_jobs[coming : coming + ORDERED_JOBS] if first >= STEPS_PER_TURN else []
             turned = [turn(job) for job in turn_jobs]
+            if first == 0:
+                build_tables()
             accs = [project(b, t) for b, t in turn_steps]
             for job, banks in zip(turn_jobs, turned):
                 pack(job, banks)
-            for job in coming_jobs:
-                put_in_order(job)
-            for (b, t), acc in zip(turn_steps, accs):
-                finish(b, t, acc)
+            for step, prod in unadded:
+                add_and_store(*step, prod, nc.vector)
+            first_prod, second_prod = [finish(b, t, acc) for (b, t), acc in zip(turn_steps, accs)]
+            add_and_store(*turn_steps[0], first_prod, nc.gpsimd)
+            unadded = [(turn_steps[1], second_prod)]
+        for step, prod in unadded:
+            add_and_store(*step, prod, nc.vector)

@@ -45,7 +45,7 @@ def tile_qwen3nextattentionforengine_pa_kernel(
 
     with ExitStack() as ctx:
         consts = ctx.enter_context(tc.tile_pool(name="consts", bufs=1))
-        raw_pool = ctx.enter_context(tc.tile_pool(name="raw", bufs=len(halves) - 2))
+        raw_pool = ctx.enter_context(tc.tile_pool(name="raw", bufs=len(halves) - 4))
         group_pool = ctx.enter_context(tc.tile_pool(name="grouped", bufs=6))
         weight_pool = ctx.enter_context(tc.tile_pool(name="weights", bufs=2))
         small_pool = ctx.enter_context(tc.tile_pool(name="small", bufs=4))
@@ -76,7 +76,7 @@ def tile_qwen3nextattentionforengine_pa_kernel(
                 if pieces == 1:
                     raw = raw_pool.tile([P, 2, HIDDEN], BF16, name="raw")
                 else:
-                    raw = consts.tile([P, 2, width], BF16, name=f"raw_{owner}_{first}")
+                    raw = consts.tile([P, 2, width], BF16, name=f"raw_{owner}_{h}_{first}")
                 nc.sync.dma_start(out=raw[:], in_=source[:, :, first : first + width])
                 words = raw[:].bitcast(F32)
                 for i in range(PASSES // pieces):
@@ -84,40 +84,46 @@ def tile_qwen3nextattentionforengine_pa_kernel(
 
         cos_sb = consts.tile([P, TOKEN_TILES, HEAD], BF16, name="cos_sb")
         sin_sb = consts.tile([P, TOKEN_TILES, HEAD], BF16, name="sin_sb")
-        load_half(*halves[0], pieces=PASSES)
-        load_half(*halves[1], pieces=2)
-        load_half(*halves[2])
-        nc.sync.dma_start(out=gain_rows[0:1, 0:HEAD], in_=q_norm_w.unsqueeze(0))
-        nc.sync.dma_start(out=gain_rows[0:1, HEAD : 2 * HEAD], in_=k_norm_w.unsqueeze(0))
+        nc.scalar.dma_start(out=gain_rows[0:1, 0:HEAD], in_=q_norm_w.unsqueeze(0))
+        nc.scalar.dma_start(out=gain_rows[0:1, HEAD : 2 * HEAD], in_=k_norm_w.unsqueeze(0))
+        for owner, h in halves[:3]:
+            load_half(owner, h, pieces=2)
         nc.sync.dma_start(out=cos_sb[:], in_=cos.rearrange("b (t p) d -> p (b t) d", p=P))
         nc.sync.dma_start(out=sin_sb[:], in_=sin.rearrange("b (t p) d -> p (b t) d", p=P))
-        for owner, h in halves[3:]:
+        load_half(*halves[3], pieces=2)
+        for owner, h in halves[4:]:
             load_half(owner, h)
 
-        tables = consts.tile([P, 2, TOKEN_TILES, 2, HEAD], F32, name="tables")
+        tables = {}
         LOW = slice(0, HEAD // 2)
         HIGH = slice(HEAD // 2, HEAD)
+        gains = consts.tile([P, 2 * HEAD], F32, name="gains")
 
-        def build_tables():
-            gains = acc_psum.tile([P, 2 * HEAD], F32, name="acc")
-            nc.tensor.matmul(out=gains[:], lhsT=ones[:], rhs=gain_rows[:], start=True, stop=True)
-            for n in range(2):
-                gain = gains[:, HEAD * n : HEAD * (n + 1)].unsqueeze(1)
-                nc.vector.tensor_tensor(
-                    out=tables[:, n, :, 0, :],
-                    in0=cos_sb[:],
-                    in1=gain.to_broadcast([P, TOKEN_TILES, HEAD]),
-                    op=ALU.mult,
+        def spread_gains():
+            spread = acc_psum.tile([P, 2 * HEAD], F32, name="acc")
+            nc.tensor.matmul(out=spread[:], lhsT=ones[:], rhs=gain_rows[:], start=True, stop=True)
+            nc.vector.tensor_copy(out=gains[:], in_=spread[:])
+
+        def build_tables(n, pair):
+            table = consts.tile([P, 2, 2, HEAD], F32, name=f"table_{n}_{pair}")
+            tiles = slice(2 * pair, 2 * pair + 2)
+            gain = gains[:, HEAD * n : HEAD * (n + 1)].unsqueeze(1)
+            nc.vector.tensor_tensor(
+                out=table[:, :, 0, :],
+                in0=cos_sb[:, tiles, :],
+                in1=gain.to_broadcast([P, 2, HEAD]),
+                op=ALU.mult,
+            )
+            for here, there, sign in ((LOW, HIGH, 1.0), (HIGH, LOW, -1.0)):
+                nc.vector.scalar_tensor_tensor(
+                    out=table[:, :, 1, here],
+                    in0=sin_sb[:, tiles, there],
+                    scalar=sign,
+                    in1=gain[:, :, here].to_broadcast([P, 2, HEAD // 2]),
+                    op0=ALU.mult,
+                    op1=ALU.mult,
                 )
-                for here, there, sign in ((LOW, HIGH, 1.0), (HIGH, LOW, -1.0)):
-                    nc.vector.scalar_tensor_tensor(
-                        out=tables[:, n, :, 1, here],
-                        in0=sin_sb[:, :, there],
-                        scalar=sign,
-                        in1=gain[:, :, here].to_broadcast([P, TOKEN_TILES, HEAD // 2]),
-                        op0=ALU.mult,
-                        op1=ALU.mult,
-                    )
+            tables[(n, pair)] = table
 
         operands = {}
         packed = set()
@@ -199,40 +205,46 @@ def tile_qwen3nextattentionforengine_pa_kernel(
                     out=prod[:, hd, :, :],
                     in0=acc[:, HEAD * hd : HEAD * (hd + 1)].unsqueeze(1).to_broadcast([P, 2, HEAD]),
                     scalar=inv_rms[:, hd : hd + 1],
-                    in1=tables[:, n, t, :, :],
+                    in1=tables[(n, t // 2)][:, t % 2, :, :],
                     op0=ALU.mult,
                     op1=ALU.mult,
                 )
-            return prod
-
-        def add_and_store(b, t, prod, engine):
-            rows, target, n = blocks[b]
-            heads = rows.shape[0] // HEAD
             result = result_pool.tile([P, heads, 2, HEAD // 2], F32, name="result")
-            stay = prod[:, :, 0, :].rearrange("p h (s d) -> p h s d", s=2)
-            cross = prod[:, :, 1, :].rearrange("p h (s d) -> p h s d", s=2)
-            engine.tensor_tensor(out=result[:], in0=stay, in1=cross[:, :, ::-1, :], op=ALU.add)
-            nc.sync.dma_start(out=target[P * t : P * (t + 1), :], in_=result[:].rearrange("p h s d -> p (h s d)"))
+            return prod, result
 
+        def add_and_store(engine, b, t, pair, first, count):
+            prod, result = pair
+            part = slice(first, first + count)
+            stay = prod[:, part, 0, :].rearrange("p h (s d) -> p h s d", s=2)
+            cross = prod[:, part, 1, :].rearrange("p h (s d) -> p h s d", s=2)
+            engine.tensor_tensor(out=result[:, part, :, :], in0=stay, in1=cross[:, :, ::-1, :], op=ALU.add)
+            nc.sync.dma_start(
+                out=blocks[b][1][P * t : P * (t + 1), HEAD * first : HEAD * (first + count)],
+                in_=result[:, part, :, :].rearrange("p h s d -> p (h s d)"),
+            )
+
+        steps = [(b, t) for b in range(len(blocks)) for t in range(TOKEN_TILES)]
         for job in jobs[:HEAD_JOBS]:
             pack(job, turn(job))
+        spread_gains()
 
         later_jobs = jobs[HEAD_JOBS:]
-        steps = [(b, t) for b in range(len(blocks)) for t in range(TOKEN_TILES)]
-        unadded = []
         for first in range(0, len(steps), STEPS_PER_TURN):
             turn_steps = steps[first : first + STEPS_PER_TURN]
             turn_jobs = later_jobs[first : first + STEPS_PER_TURN]
             turned = [turn(job) for job in turn_jobs]
-            if first == 0:
-                build_tables()
+            for b, t in (steps[first], steps[min(first + 2 * STEPS_PER_TURN, len(steps) - 2)]):
+                if (blocks[b][2], t // 2) not in tables:
+                    build_tables(blocks[b][2], t // 2)
             accs = [project(b, t) for b, t in turn_steps]
             for job, banks in zip(turn_jobs, turned):
                 pack(job, banks)
-            for step, prod in unadded:
-                add_and_store(*step, prod, nc.vector)
-            first_prod, second_prod = [finish(b, t, acc) for (b, t), acc in zip(turn_steps, accs)]
-            add_and_store(*turn_steps[0], first_prod, nc.gpsimd)
-            unadded = [(turn_steps[1], second_prod)]
-        for step, prod in unadded:
-            add_and_store(*step, prod, nc.vector)
+            pairs = [finish(b, t, acc) for (b, t), acc in zip(turn_steps, accs)]
+            if turn_steps[1] != steps[-1]:
+                for (b, t), pair in zip(turn_steps, pairs):
+                    add_and_store(nc.gpsimd, b, t, pair, 0, blocks[b][0].shape[0] // HEAD)
+            else:
+                add_and_store(nc.gpsimd, *turn_steps[0], pairs[0], 0, 2)
+                add_and_store(nc.vector, *turn_steps[0], pairs[0], 2, 2)
+                add_and_store(nc.vector, *turn_steps[1], pairs[1], 0, 2)
+                add_and_store(nc.vector, *turn_steps[1], pairs[1], 2, 2)

from contextlib import ExitStack

import concourse.mybir as mybir
from concourse.masks import make_identity

F32 = mybir.dt.float32
BF16 = mybir.dt.bfloat16
U32 = mybir.dt.uint32
U8 = mybir.dt.uint8
FP8X4 = mybir.dt.float8_e4m3fn_x4
ACT = mybir.ActivationFunctionType
ALU = mybir.AluOpType

P = 128
PACK = 4
HIDDEN = 2048
PASSES = HIDDEN // (P * PACK)
BLOCK = 512
HALF = BLOCK // 2
HEAD = 128
TOKEN_TILES = 4
EPS = 1e-6
STEPS_PER_TURN = 2

FLOPS = 2 * 512 * (2048 + 512) * HIDDEN


def tile_qwen3nextattentionforengine_pa_kernel(
    tc, hidden_states, cos, sin, Wq_query, Wk, q_norm_w, k_norm_w, out_0, out_1
):
    nc = tc.nc
    tokens = hidden_states.rearrange("b s k -> (b s) k")
    q_flat = out_0.rearrange("b s h d -> (b s) (h d)")
    k_flat = out_1.rearrange("b s h d -> (b s) (h d)")

    blocks = []
    for first, width in ((0, HALF), (HALF, HALF), (512, BLOCK), (1024, BLOCK), (1536, BLOCK)):
        blocks.append((Wq_query[first : first + width, :], q_flat[:, first : first + width], 0))
    blocks.append((Wk, k_flat, 1))

    halves = [("x", 0), (0, 0), ("x", 1), (1, 0)]
    halves += [(b, h) for b in range(2, len(blocks)) for h in range(2)]
    jobs = [(owner, h, g) for owner, h in halves for g in (0, 2)]
    HEAD_JOBS = 4

    with ExitStack() as ctx:
        consts = ctx.enter_context(tc.tile_pool(name="consts", bufs=1))
        raw_pool = ctx.enter_context(tc.tile_pool(name="raw", bufs=len(halves) - 4))
        group_pool = ctx.enter_context(tc.tile_pool(name="grouped", bufs=6))
        weight_pool = ctx.enter_context(tc.tile_pool(name="weights", bufs=2))
        small_pool = ctx.enter_context(tc.tile_pool(name="small", bufs=4))
        prod_pool = ctx.enter_context(tc.tile_pool(name="prod", bufs=4))
        result_pool = ctx.enter_context(tc.tile_pool(name="result", bufs=len(blocks) * TOKEN_TILES))
        turn_psum = ctx.enter_context(tc.psum_pool(name="turn", bufs=4))
        acc_psum = ctx.enter_context(tc.psum_pool(name="acc", bufs=4))
        ctx.enter_context(tc.manual_schedule())

        eps_col = consts.tile([P, 1], F32, name="eps_col")
        nc.vector.memset(eps_col[:], EPS)
        gain_rows = consts.tile([P, 2 * HEAD], BF16, name="gain_rows")
        nc.vector.memset(gain_rows[:], 0.0)
        ones = consts.tile([P, P], BF16, name="ones")
        nc.vector.memset(ones[:], 1.0)
        ident = consts.tile([P, P], F32, name="ident")
        make_identity(nc, ident[:])
        warm = consts.tile([P, 1], F32, name="warm")
        nc.scalar.activation(out=warm[:], in_=eps_col[:], func=ACT.Abs_reciprocal_sqrt)

        raws = {}

        def load_half(owner, h, pieces=1):
            rows = tokens if owner == "x" else blocks[owner][0]
            source = rows[HALF * h : HALF * (h + 1), :].rearrange("(r p) k -> p r k", r=2)
            width = HIDDEN // pieces
            for first in range(0, HIDDEN, width):
                if pieces == 1:
                    raw = raw_pool.tile([P, 2, HIDDEN], BF16, name="raw")
                else:
                    raw = consts.tile([P, 2, width], BF16, name=f"raw_{owner}_{h}_{first}")
                nc.sync.dma_start(out=raw[:], in_=source[:, :, first : first + width])
                words = raw[:].bitcast(F32)
                for i in range(PASSES // pieces):
                    raws[(owner, h, first // (P * PACK) + i)] = words[:, :, 2 * P * i : 2 * P * (i + 1)]

        cos_sb = consts.tile([P, TOKEN_TILES, HEAD], BF16, name="cos_sb")
        sin_sb = consts.tile([P, TOKEN_TILES, HEAD], BF16, name="sin_sb")
        nc.scalar.dma_start(out=gain_rows[0:1, 0:HEAD], in_=q_norm_w.unsqueeze(0))
        nc.scalar.dma_start(out=gain_rows[0:1, HEAD : 2 * HEAD], in_=k_norm_w.unsqueeze(0))
        for owner, h in halves[:3]:
            load_half(owner, h, pieces=2)
        nc.sync.dma_start(out=cos_sb[:], in_=cos.rearrange("b (t p) d -> p (b t) d", p=P))
        nc.sync.dma_start(out=sin_sb[:], in_=sin.rearrange("b (t p) d -> p (b t) d", p=P))
        load_half(*halves[3], pieces=2)
        for owner, h in halves[4:]:
            load_half(owner, h)

        tables = {}
        LOW = slice(0, HEAD // 2)
        HIGH = slice(HEAD // 2, HEAD)
        gains = consts.tile([P, 2 * HEAD], F32, name="gains")

        def spread_gains():
            spread = acc_psum.tile([P, 2 * HEAD], F32, name="acc")
            nc.tensor.matmul(out=spread[:], lhsT=ones[:], rhs=gain_rows[:], start=True, stop=True)
            nc.vector.tensor_copy(out=gains[:], in_=spread[:])

        def build_tables(n, pair):
            table = consts.tile([P, 2, 2, HEAD], F32, name=f"table_{n}_{pair}")
            tiles = slice(2 * pair, 2 * pair + 2)
            gain = gains[:, HEAD * n : HEAD * (n + 1)].unsqueeze(1)
            nc.vector.tensor_tensor(
                out=table[:, :, 0, :],
                in0=cos_sb[:, tiles, :],
                in1=gain.to_broadcast([P, 2, HEAD]),
                op=ALU.mult,
            )
            for here, there, sign in ((LOW, HIGH, 1.0), (HIGH, LOW, -1.0)):
                nc.vector.scalar_tensor_tensor(
                    out=table[:, :, 1, here],
                    in0=sin_sb[:, tiles, there],
                    scalar=sign,
                    in1=gain[:, :, here].to_broadcast([P, 2, HEAD // 2]),
                    op0=ALU.mult,
                    op1=ALU.mult,
                )
            tables[(n, pair)] = table

        operands = {}
        packed = set()

        def turn(job):
            owner, h, first_pass = job
            if owner not in operands:
                pool = consts if owner == "x" else weight_pool
                codes = pool.tile([P, PASSES, BLOCK], U32, align_bytes=64, name="codes")
                scales = pool.tile([P, PASSES, BLOCK], U8, align_bytes=64, name="scales")
                operands[owner] = (codes, scales)
            banks = []
            for g in (first_pass, first_pass + 1):
                bank = turn_psum.tile([P, 2, 2, P], F32, name="bank")
                for u in range(2):
                    for r in range(2):
                        picked = raws[(owner, h, g)][:, r, u : 2 * P : 2]
                        nc.tensor.transpose(bank[:, u, r, :], picked, ident[:])
                banks.append(bank)
            return banks

        def pack(job, banks):
            owner, h, first_pass = job
            codes, scales = operands[owner]
            rows = slice(HALF * h, HALF * (h + 1))
            grouped_pair = []
            for bank in banks:
                grouped = group_pool.tile([P, PACK * HALF], BF16, align_bytes=64, name="grouped")
                nc.scalar.copy(
                    out=grouped[:].bitcast(F32).rearrange("p (r c u) -> p r c u", r=2, u=2),
                    in_=bank[:].rearrange("p u r c -> p r c u"),
                )
                grouped_pair.append(grouped)
            for g, grouped in zip((first_pass, first_pass + 1), grouped_pair):
                nc.vector.quantize_mx(
                    out=codes[:, g, rows].bitcast(FP8X4), scales=scales[:, g, rows], in_=grouped[:]
                )
            packed.add(job)

        def project(b, t):
            width = blocks[b][0].shape[0]
            needed = [("x", t // 2, g) for g in (0, 2)]
            needed += [(b, h, g) for h in range(width // HALF) for g in (0, 2)]
            assert all(job in packed for job in needed)
            x_codes, x_scales = operands["x"]
            w_codes, w_scales = operands[b]
            toks = slice(P * t, P * (t + 1))
            acc = acc_psum.tile([P, width], F32, name="acc")
            for g in range(PASSES):
                nc.tensor.matmul_mx(
                    out=acc[:],
                    lhsT=x_codes[:, g, toks].bitcast(FP8X4),
                    lhsT_scale=x_scales[:, g, toks],
                    rhs=w_codes[:, g, 0:width].bitcast(FP8X4),
                    rhs_scale=w_scales[:, g, 0:width],
                    start=(g == 0),
                    stop=(g == PASSES - 1),
                )
            return acc

        def finish(b, t, acc):
            rows, target, n = blocks[b]
            width = rows.shape[0]
            heads = width // HEAD
            squares = small_pool.tile([P, width], BF16, name="squares")
            sums = small_pool.tile([P, heads], F32, name="sums")
            for hd in range(heads):
                cols = slice(HEAD * hd, HEAD * (hd + 1))
                nc.scalar.activation(
                    out=squares[:, cols], in_=acc[:, cols], func=ACT.Square, accum_out=sums[:, hd : hd + 1]
                )
            inv_rms = small_pool.tile([P, heads], F32, name="inv_rms")
            nc.scalar.activation(
                out=inv_rms[:], in_=sums[:], func=ACT.Abs_reciprocal_sqrt, bias=eps_col[:], scale=1.0 / HEAD
            )
            prod = prod_pool.tile([P, heads, 2, HEAD], F32, name="prod")
            for hd in range(heads):
                nc.vector.scalar_tensor_tensor(
                    out=prod[:, hd, :, :],
                    in0=acc[:, HEAD * hd : HEAD * (hd + 1)].unsqueeze(1).to_broadcast([P, 2, HEAD]),
                    scalar=inv_rms[:, hd : hd + 1],
                    in1=tables[(n, t // 2)][:, t % 2, :, :],
                    op0=ALU.mult,
                    op1=ALU.mult,
                )
            result = result_pool.tile([P, heads, 2, HEAD // 2], F32, name="result")
            return prod, result

        def add_and_store(engine, b, t, pair, first, count):
            prod, result = pair
            part = slice(first, first + count)
            stay = prod[:, part, 0, :].rearrange("p h (s d) -> p h s d", s=2)
            cross = prod[:, part, 1, :].rearrange("p h (s d) -> p h s d", s=2)
            engine.tensor_tensor(out=result[:, part, :, :], in0=stay, in1=cross[:, :, ::-1, :], op=ALU.add)
            nc.sync.dma_start(
                out=blocks[b][1][P * t : P * (t + 1), HEAD * first : HEAD * (first + count)],
                in_=result[:, part, :, :].rearrange("p h s d -> p (h s d)"),
            )

        steps = [(b, t) for b in range(len(blocks)) for t in range(TOKEN_TILES)]
        for job in jobs[:HEAD_JOBS]:
            pack(job, turn(job))
        spread_gains()

        later_jobs = jobs[HEAD_JOBS:]
        for first in range(0, len(steps), STEPS_PER_TURN):
            turn_steps = steps[first : first + STEPS_PER_TURN]
            turn_jobs = later_jobs[first : first + STEPS_PER_TURN]
            turned = [turn(job) for job in turn_jobs]
            for b, t in (steps[first], steps[min(first + 2 * STEPS_PER_TURN, len(steps) - 2)]):
                if (blocks[b][2], t // 2) not in tables:
                    build_tables(blocks[b][2], t // 2)
            accs = [project(b, t) for b, t in turn_steps]
            for job, banks in zip(turn_jobs, turned):
                pack(job, banks)
            pairs = [finish(b, t, acc) for (b, t), acc in zip(turn_steps, accs)]
            if turn_steps[1] != steps[-1]:
                for (b, t), pair in zip(turn_steps, pairs):
                    add_and_store(nc.gpsimd, b, t, pair, 0, blocks[b][0].shape[0] // HEAD)
            else:
                add_and_store(nc.gpsimd, *turn_steps[0], pairs[0], 0, 2)
                add_and_store(nc.vector, *turn_steps[0], pairs[0], 2, 2)
                add_and_store(nc.vector, *turn_steps[1], pairs[1], 0, 2)
                add_and_store(nc.vector, *turn_steps[1], pairs[1], 2, 2)
